import numpy as np
import ml_dtypes


def mxq(x, axis, fmt="e4m3"):
    dtype, down = {"e4m3": (ml_dtypes.float8_e4m3fn, 7), "e5m2": (ml_dtypes.float8_e5m2, 14)}[fmt]
    v = np.moveaxis(np.asarray(x, np.float32).astype(ml_dtypes.bfloat16).astype(np.float64), axis, -1)
    blocks = v.reshape(v.shape[:-1] + (-1, 32))
    amax = np.abs(blocks).max(-1, keepdims=True)
    byte = np.maximum(np.where(amax > 0, np.frexp(amax)[1] - 1 + 127, 0) - down, 1)
    scale = np.exp2(byte - 127.0)
    codes = (blocks / scale).astype(np.float32).astype(dtype).astype(np.float64)
    return np.moveaxis((codes * scale).reshape(v.shape), -1, axis)


WIDE = False


def mx_kscale(k):
    if not WIDE:
        return np.ones(k)
    levels = np.array([20, -20, 10, -10, 0])
    a = np.random.permutation(np.resize(levels, k // 512 * 4)).reshape(k // 512, 4)
    idx = np.arange(k)
    return np.exp2(a[idx // 512, idx % 128 // 32])


BF16 = ml_dtypes.bfloat16


def bf(x):
    return np.asarray(x, np.float32).astype(BF16)


def f64(x):
    return np.asarray(x).astype(np.float64)


B, IN_DIM, LAT, OUT_DIM = 2048, 512, 1024, 512
G = IN_DIM + LAT


def sigmoid(v):
    return 1.0 / (1.0 + np.exp(-v))


def setup_inputs():
    u = mx_kscale(OUT_DIM)
    x_t = bf(np.random.standard_normal((B, IN_DIM)))
    h_t = bf(np.random.standard_normal((B, LAT)) * 0.85)
    Wy0 = bf(np.random.standard_normal((G, OUT_DIM)) * 0.8 / np.sqrt(G))
    by = bf(np.random.standard_normal(OUT_DIM) * 0.2)
    Wo0 = bf(np.random.standard_normal((G, OUT_DIM)) * 0.8 / np.sqrt(G))
    bo = bf(np.random.standard_normal(OUT_DIM) * 0.2)
    g = bf(np.random.standard_normal((B, OUT_DIM)) * np.exp2(np.random.randint(-12, 1, (B, 1))) * 32.0 * u)
    xh = np.concatenate([f64(x_t), f64(h_t)], axis=1)
    y_hat = np.tanh(xh @ f64(Wy0) + f64(by))
    o_t = sigmoid(xh @ f64(Wo0) + f64(bo))
    return {
        "x_t": x_t,
        "h_t": h_t,
        "Wy": bf(f64(Wy0) / u),
        "by": by,
        "Wo": bf(f64(Wo0) / u),
        "bo": bo,
        "y_hat": np.asarray(y_hat, np.float32),
        "o_t": np.asarray(o_t, np.float32),
        "grad_out": g,
    }


def reference(x_t, h_t, Wy, by, Wo, bo, y_hat, o_t, grad_out):
    g = f64(grad_out)
    y = f64(y_hat)
    o = f64(o_t)
    dzy = g * o * (1.0 - y * y)
    dzo = g * y * o * (1.0 - o)
    wy_x = f64(Wy)[:IN_DIM]
    wo_x = f64(Wo)[:IN_DIM]
    py = mxq(dzy, 1, "e5m2") @ mxq(wy_x, 1, "e4m3").T
    po = mxq(dzo, 1, "e5m2") @ mxq(wo_x, 1, "e4m3").T
    return py + po

@@ -1,0 +1,200 @@
+from contextlib import ExitStack
+
+import concourse.mybir as mybir
+from concourse.masks import make_identity
+
+F32 = mybir.dt.float32
+BF16 = mybir.dt.bfloat16
+U32 = mybir.dt.uint32
+U8 = mybir.dt.uint8
+E5M2X4 = mybir.dt.float8_e5m2_x4
+E4M3X4 = mybir.dt.float8_e4m3fn_x4
+ALU = mybir.AluOpType
+ACT = mybir.ActivationFunctionType
+
+P = 128
+PACK = 4
+B = 2048
+K = P * PACK
+N = 512
+SLOTS = B // P
+PAIRS = SLOTS // 2
+W_PIECES = 4
+FIRST_W_STEP = 3
+FIRST_PRODUCT_STEP = FIRST_W_STEP + W_PIECES + 1
+
+FLOPS = 2 * 2 * B * K * N
+BYTES = B * K * (2 + 4 + 4) + 2 * N * K * 2 + B * N * 4
+
+
+def tile_gatel0rdcell_pb_v_kernel(tc, x_t, h_t, Wy, by, Wo, bo, y_hat, o_t, grad_out, out):
+    nc = tc.nc
+    y_rows = y_hat.rearrange("(p s) k -> p s k", s=SLOTS)
+    o_rows = o_t.rearrange("(p s) k -> p s k", s=SLOTS)
+    g_rows = grad_out.rearrange("(p s) k -> p s k", s=SLOTS)
+    out_rows = out.rearrange("(p s) n -> p s n", s=SLOTS)
+
+    with ExitStack() as stack:
+        const = stack.enter_context(tc.tile_pool(name="const", bufs=1))
+        inputs = stack.enter_context(tc.tile_pool(name="inputs", bufs=1))
+        work = stack.enter_context(tc.tile_pool(name="work", bufs=3))
+        codes_pool = stack.enter_context(tc.tile_pool(name="codes", bufs=PAIRS))
+        results = stack.enter_context(tc.tile_pool(name="results", bufs=PAIRS))
+        psum = stack.enter_context(tc.psum_pool(name="psum", bufs=2))
+
+        ident_f32 = const.tile([P, P], F32, name="ident_f32")
+        make_identity(nc, ident_f32[:])
+        ident_bf16 = const.tile([P, P], BF16, name="ident_bf16")
+        make_identity(nc, ident_bf16[:])
+
+        y_in, o_in, g_in = {}, {}, {}
+
+        def load_slots(first, count):
+            g_tile = inputs.tile([P, count, K], BF16, name="g%d" % first)
+            o_tile = inputs.tile([P, count, K], F32, name="o%d" % first)
+            y_tile = inputs.tile([P, count, K], F32, name="y%d" % first)
+            nc.sync.dma_start(out=g_tile[:], in_=g_rows[:, first : first + count, :])
+            nc.sync.dma_start(out=o_tile[:], in_=o_rows[:, first : first + count, :])
+            nc.sync.dma_start(out=y_tile[:], in_=y_rows[:, first : first + count, :])
+            for j in range(count):
+                g_in[first + j] = g_tile[:, j, :]
+                o_in[first + j] = o_tile[:, j, :]
+                y_in[first + j] = y_tile[:, j, :]
+
+        w_raw = []
+
+        def load_weights():
+            for name, w in (("wy_raw", Wy), ("wo_raw", Wo)):
+                raw = const.tile([P, K * N // (P * P), P], BF16, name=name)
+                quarters = w[0:N, :].rearrange("i (t c) -> (i t) c", t=PACK)
+                nc.sync.dma_start(out=raw[:], in_=quarters.rearrange("(n p) c -> p n c", p=P))
+                w_raw.append(raw)
+
+        load_slots(0, 1)
+        load_slots(1, 1)
+        load_slots(2, 2)
+        load_weights()
+        for first in range(4, SLOTS, 2):
+            load_slots(first, 2)
+
+        w_grouped = const.tile([P, 2 * N * PACK], BF16, name="w_grouped", align_bytes=64)
+        w_codes = const.tile([P, 2 * N], U32, name="w_codes", align_bytes=64)
+        w_scales = const.tile([P, 2 * N], U8, name="w_scales", align_bytes=64)
+
+        def transpose_weight_piece(piece):
+            z, part = divmod(piece, 2)
+            w_t = psum.tile([P, 8, P], BF16, name="w_t", tag="acc")
+            for n in range(8):
+                nc.tensor.transpose(out=w_t[:, n, :], in_=w_raw[z][:, 8 * part + n, :], identity=ident_bf16[:])
+            nc.scalar.copy(
+                out=w_grouped[:, piece * 8 * P : (piece + 1) * 8 * P],
+                in_=w_t[:].rearrange("p n c -> p (n c)"),
+            )
+
+        def quantise_weights():
+            nc.vector.quantize_mx(out=w_codes[:].bitcast(E4M3X4), scales=w_scales[:], in_=w_grouped[:])
+
+        go_nat, y_t, o_t_ps, go_t, y_sb, ysq_sb = {}, {}, {}, {}, {}, {}
+        grouped, dz_codes, dz_scales, acc = {}, {}, {}, {}
+
+        def gate_product(s):
+            go_nat[s] = work.tile([P, K], F32, name="go_nat", bufs=4)
+            nc.gpsimd.tensor_tensor(out=go_nat[s][:], in0=g_in[s], in1=o_in[s], op=ALU.mult)
+
+        def transpose_slot(s):
+            y_t[s] = psum.tile([P, PACK, P], F32, name="y_t")
+            o_t_ps[s] = psum.tile([P, PACK, P], F32, name="o_t_ps")
+            go_t[s] = psum.tile([P, PACK, P], F32, name="go_t")
+            for dst, src in ((y_t[s], y_in[s]), (o_t_ps[s], o_in[s]), (go_t[s], go_nat[s])):
+                for t in range(PACK):
+                    nc.tensor.transpose(out=dst[:, t, :], in_=src[:, t * P : (t + 1) * P], identity=ident_f32[:])
+
+        def scalar_parts(s):
+            y_sb[s] = work.tile([P, P, PACK], F32, name="y_sb")
+            ysq_sb[s] = work.tile([P, P, PACK], F32, name="ysq_sb")
+            y_view = y_t[s][:].rearrange("p t b -> p b t")
+            nc.scalar.copy(out=y_sb[s][:], in_=y_view)
+            nc.scalar.activation(out=ysq_sb[s][:], in_=y_view, func=ACT.Square)
+
+        def gradients(s):
+            q, half = divmod(s, 2)
+            if half == 0:
+                grouped[q] = work.tile([P, 2, 2, P, PACK], BF16, name="grouped", align_bytes=64)
+            go_view = go_t[s][:].rearrange("p t b -> p b t")
+            yo = work.tile([P, P, PACK], F32, name="yo")
+            nc.vector.scalar_tensor_tensor(
+                out=yo[:], in0=o_t_ps[s][:].rearrange("p t b -> p b t"), scalar=1.0, in1=y_sb[s][:],
+                op0=ALU.subtract, op1=ALU.mult,
+            )
+            nc.vector.scalar_tensor_tensor(
+                out=grouped[q][:, half, 0], in0=ysq_sb[s][:], scalar=1.0, in1=go_view,
+                op0=ALU.subtract, op1=ALU.mult,
+            )
+            nc.vector.tensor_tensor(out=grouped[q][:, half, 1], in0=yo[:], in1=go_view, op=ALU.mult)
+
+        def quantise_pair(q):
+            dz_codes[q] = codes_pool.tile([P, 4 * P], U32, name="dz_codes", align_bytes=64)
+            dz_scales[q] = codes_pool.tile([P, 4 * P], U8, name="dz_scales", align_bytes=64)
+            nc.vector.quantize_mx(
+                out=dz_codes[q][:].bitcast(E5M2X4),
+                scales=dz_scales[q][:],
+                in_=grouped[q][:].rearrange("p h z b t -> p (h z b t)"),
+            )
+
+        def multiply_pair(q):
+            for half in range(2):
+                acc[2 * q + half] = psum.tile([P, N], F32, name="acc")
+                for z in range(2):
+                    cols = slice((2 * half + z) * P, (2 * half + z + 1) * P)
+                    w_cols = slice(z * N, (z + 1) * N)
+                    nc.tensor.matmul_mx(
+                        out=acc[2 * q + half][:],
+                        lhsT=dz_codes[q][:, cols].bitcast(E5M2X4),
+                        lhsT_scale=dz_scales[q][:, cols],
+                        rhs=w_codes[:, w_cols].bitcast(E4M3X4),
+                        rhs_scale=w_scales[:, w_cols],
+                        start=(z == 0),
+                        stop=(z == 1),
+                    )
+
+        def store_pair(q):
+            out_sb = results.tile([P, 2, N], F32, name="out_sb")
+            for half in range(2):
+                nc.scalar.mul(out=out_sb[:, half, :], in_=acc[2 * q + half][:], mul=-1.0)
+            nc.sync.dma_start(out=out_rows[:, 2 * q : 2 * q + 2, :], in_=out_sb[:])
+
+        gate_product(0)
+        gate_product(1)
+        transpose_slot(0)
+        scalar_parts(0)
+        quantised = 0
+        multiplied = 0
+        stored = 0
+        for s in range(SLOTS):
+            if s + 2 < SLOTS:
+                gate_product(s + 2)
+            if s + 1 < SLOTS:
+                transpose_slot(s + 1)
+                scalar_parts(s + 1)
+            if FIRST_W_STEP <= s < FIRST_W_STEP + W_PIECES:
+                transpose_weight_piece(s - FIRST_W_STEP)
+            if stored < multiplied:
+                store_pair(stored)
+                stored += 1
+            gradients(s)
+            if s == FIRST_W_STEP + W_PIECES:
+                quantise_weights()
+            if s >= 2 and s % 2 == 0:
+                quantise_pair(quantised)
+                quantised += 1
+            if s >= FIRST_PRODUCT_STEP and multiplied < quantised:
+                multiply_pair(multiplied)
+                multiplied += 1
+        quantise_pair(quantised)
+        quantised += 1
+        while stored < PAIRS:
+            if multiplied < PAIRS:
+                multiply_pair(multiplied)
+                multiplied += 1
+            store_pair(stored)
+            stored += 1

@@ -99,7 +99,7 @@ def tile_gatel0rdcell_pb_v_kernel(tc, x_t, h_t, Wy, by, Wo, bo, y_hat, o_t, grad
 
         def gate_product(s):
             go_nat[s] = work.tile([P, K], F32, name="go_nat", bufs=4)
-            nc.gpsimd.tensor_tensor(out=go_nat[s][:], in0=g_in[s], in1=o_in[s], op=ALU.mult)
+            nc.vector.tensor_tensor(out=go_nat[s][:], in0=g_in[s], in1=o_in[s], op=ALU.mult)
 
         def transpose_slot(s):
             y_t[s] = psum.tile([P, PACK, P], F32, name="y_t")

@@ -19,9 +19,6 @@ K = P * PACK
 N = 512
 SLOTS = B // P
 PAIRS = SLOTS // 2
-W_PIECES = 4
-FIRST_W_STEP = 3
-FIRST_PRODUCT_STEP = FIRST_W_STEP + W_PIECES + 1
 
 FLOPS = 2 * 2 * B * K * N
 BYTES = B * K * (2 + 4 + 4) + 2 * N * K * 2 + B * N * 4
@@ -38,14 +35,21 @@ def tile_gatel0rdcell_pb_v_kernel(tc, x_t, h_t, Wy, by, Wo, bo, y_hat, o_t, grad
         const = stack.enter_context(tc.tile_pool(name="const", bufs=1))
         inputs = stack.enter_context(tc.tile_pool(name="inputs", bufs=1))
         work = stack.enter_context(tc.tile_pool(name="work", bufs=3))
-        codes_pool = stack.enter_context(tc.tile_pool(name="codes", bufs=PAIRS))
-        results = stack.enter_context(tc.tile_pool(name="results", bufs=PAIRS))
+        codes_pool = stack.enter_context(tc.tile_pool(name="codes", bufs=3))
+        results = stack.enter_context(tc.tile_pool(name="results", bufs=SLOTS))
         psum = stack.enter_context(tc.psum_pool(name="psum", bufs=2))
+        stack.enter_context(tc.manual_schedule())
 
-        ident_f32 = const.tile([P, P], F32, name="ident_f32")
-        make_identity(nc, ident_f32[:])
         ident_bf16 = const.tile([P, P], BF16, name="ident_bf16")
         make_identity(nc, ident_bf16[:])
+        ident_f32 = const.tile([P, P], F32, name="ident_f32")
+        make_identity(nc, ident_f32[:])
+
+        w_raw = []
+        for name, w in (("wy_raw", Wy), ("wo_raw", Wo)):
+            raw = const.tile([P, N // P, K], BF16, name=name)
+            nc.sync.dma_start(out=raw[:], in_=w[0:N, :].rearrange("(c i) k -> i c k", i=P))
+            w_raw.append(raw)
 
         y_in, o_in, g_in = {}, {}, {}
 
@@ -61,53 +65,58 @@ def tile_gatel0rdcell_pb_v_kernel(tc, x_t, h_t, Wy, by, Wo, bo, y_hat, o_t, grad
                 o_in[first + j] = o_tile[:, j, :]
                 y_in[first + j] = y_tile[:, j, :]
 
-        w_raw = []
-
-        def load_weights():
-            for name, w in (("wy_raw", Wy), ("wo_raw", Wo)):
-                raw = const.tile([P, K * N // (P * P), P], BF16, name=name)
-                quarters = w[0:N, :].rearrange("i (t c) -> (i t) c", t=PACK)
-                nc.sync.dma_start(out=raw[:], in_=quarters.rearrange("(n p) c -> p n c", p=P))
-                w_raw.append(raw)
-
         load_slots(0, 1)
         load_slots(1, 1)
-        load_slots(2, 2)
-        load_weights()
-        for first in range(4, SLOTS, 2):
+        for first in range(2, SLOTS, 2):
             load_slots(first, 2)
 
-        w_grouped = const.tile([P, 2 * N * PACK], BF16, name="w_grouped", align_bytes=64)
+        w_grouped = const.tile([P, 2, N // P, P, PACK], BF16, name="w_grouped", align_bytes=64)
         w_codes = const.tile([P, 2 * N], U32, name="w_codes", align_bytes=64)
         w_scales = const.tile([P, 2 * N], U8, name="w_scales", align_bytes=64)
+        for z in range(2):
+            for part in range(2):
+                w_t = psum.tile([P, 2, PACK, P], BF16, name="w_t", tag=("y_t", "o_t_ps")[z])
+                for h in range(2):
+                    for t in range(PACK):
+                        nc.tensor.transpose(
+                            out=w_t[:, h, t, :],
+                            in_=w_raw[z][:, 2 * part + h, t * P : (t + 1) * P],
+                            identity=ident_bf16[:],
+                        )
+                dst = w_grouped[:, z, 2 * part : 2 * part + 2]
+                src = w_t[:].rearrange("p h t i -> p h i t")
+                if part == 0:
+                    nc.scalar.copy(out=dst, in_=src)
+                else:
+                    nc.vector.tensor_copy(out=dst, in_=src)
+        nc.vector.quantize_mx(
+            out=w_codes[:].bitcast(E4M3X4),
+            scales=w_scales[:],
+            in_=w_grouped[:].rearrange("p z c i t -> p (z c i t)"),
+        )
 
-        def transpose_weight_piece(piece):
-            z, part = divmod(piece, 2)
-            w_t = psum.tile([P, 8, P], BF16, name="w_t", tag="acc")
-            for n in range(8):
-                nc.tensor.transpose(out=w_t[:, n, :], in_=w_raw[z][:, 8 * part + n, :], identity=ident_bf16[:])
-            nc.scalar.copy(
-                out=w_grouped[:, piece * 8 * P : (piece + 1) * 8 * P],
-                in_=w_t[:].rearrange("p n c -> p (n c)"),
-            )
-
-        def quantise_weights():
-            nc.vector.quantize_mx(out=w_codes[:].bitcast(E4M3X4), scales=w_scales[:], in_=w_grouped[:])
-
-        go_nat, y_t, o_t_ps, go_t, y_sb, ysq_sb = {}, {}, {}, {}, {}, {}
+        go_nat, y_t, o_t_ps, go_t, y_sb, ysq_sb, yo = {}, {}, {}, {}, {}, {}, {}
         grouped, dz_codes, dz_scales, acc = {}, {}, {}, {}
+
+        def transpose_to(dst, src):
+            for t in range(PACK):
+                nc.tensor.transpose(out=dst[:, t, :], in_=src[:, t * P : (t + 1) * P], identity=ident_f32[:])
 
         def gate_product(s):
             go_nat[s] = work.tile([P, K], F32, name="go_nat", bufs=4)
-            nc.vector.tensor_tensor(out=go_nat[s][:], in0=g_in[s], in1=o_in[s], op=ALU.mult)
+            nc.gpsimd.tensor_tensor(out=go_nat[s][:], in0=g_in[s], in1=o_in[s], op=ALU.mult)
 
-        def transpose_slot(s):
+        def transpose_y(s):
             y_t[s] = psum.tile([P, PACK, P], F32, name="y_t")
+            transpose_to(y_t[s], y_in[s])
+
+        def transpose_o(s):
             o_t_ps[s] = psum.tile([P, PACK, P], F32, name="o_t_ps")
+            transpose_to(o_t_ps[s], o_in[s])
+
+        def transpose_go(s):
             go_t[s] = psum.tile([P, PACK, P], F32, name="go_t")
-            for dst, src in ((y_t[s], y_in[s]), (o_t_ps[s], o_in[s]), (go_t[s], go_nat[s])):
-                for t in range(PACK):
-                    nc.tensor.transpose(out=dst[:, t, :], in_=src[:, t * P : (t + 1) * P], identity=ident_f32[:])
+            transpose_to(go_t[s], go_nat[s])
 
         def scalar_parts(s):
             y_sb[s] = work.tile([P, P, PACK], F32, name="y_sb")
@@ -116,21 +125,23 @@ def tile_gatel0rdcell_pb_v_kernel(tc, x_t, h_t, Wy, by, Wo, bo, y_hat, o_t, grad
             nc.scalar.copy(out=y_sb[s][:], in_=y_view)
             nc.scalar.activation(out=ysq_sb[s][:], in_=y_view, func=ACT.Square)
 
+        def gate_factor(s):
+            yo[s] = work.tile([P, P, PACK], F32, name="yo")
+            nc.vector.scalar_tensor_tensor(
+                out=yo[s][:], in0=o_t_ps[s][:].rearrange("p t b -> p b t"), scalar=1.0, in1=y_sb[s][:],
+                op0=ALU.subtract, op1=ALU.mult,
+            )
+
         def gradients(s):
             q, half = divmod(s, 2)
             if half == 0:
                 grouped[q] = work.tile([P, 2, 2, P, PACK], BF16, name="grouped", align_bytes=64)
             go_view = go_t[s][:].rearrange("p t b -> p b t")
-            yo = work.tile([P, P, PACK], F32, name="yo")
-            nc.vector.scalar_tensor_tensor(
-                out=yo[:], in0=o_t_ps[s][:].rearrange("p t b -> p b t"), scalar=1.0, in1=y_sb[s][:],
-                op0=ALU.subtract, op1=ALU.mult,
-            )
             nc.vector.scalar_tensor_tensor(
                 out=grouped[q][:, half, 0], in0=ysq_sb[s][:], scalar=1.0, in1=go_view,
                 op0=ALU.subtract, op1=ALU.mult,
             )
-            nc.vector.tensor_tensor(out=grouped[q][:, half, 1], in0=yo[:], in1=go_view, op=ALU.mult)
+            nc.vector.tensor_tensor(out=grouped[q][:, half, 1], in0=yo[s][:], in1=go_view, op=ALU.mult)
 
         def quantise_pair(q):
             dz_codes[q] = codes_pool.tile([P, 4 * P], U32, name="dz_codes", align_bytes=64)
@@ -141,60 +152,57 @@ def tile_gatel0rdcell_pb_v_kernel(tc, x_t, h_t, Wy, by, Wo, bo, y_hat, o_t, grad
                 in_=grouped[q][:].rearrange("p h z b t -> p (h z b t)"),
             )
 
-        def multiply_pair(q):
-            for half in range(2):
-                acc[2 * q + half] = psum.tile([P, N], F32, name="acc")
-                for z in range(2):
-                    cols = slice((2 * half + z) * P, (2 * half + z + 1) * P)
-                    w_cols = slice(z * N, (z + 1) * N)
-                    nc.tensor.matmul_mx(
-                        out=acc[2 * q + half][:],
-                        lhsT=dz_codes[q][:, cols].bitcast(E5M2X4),
-                        lhsT_scale=dz_scales[q][:, cols],
-                        rhs=w_codes[:, w_cols].bitcast(E4M3X4),
-                        rhs_scale=w_scales[:, w_cols],
-                        start=(z == 0),
-                        stop=(z == 1),
-                    )
+        def multiply(s):
+            q, half = divmod(s, 2)
+            acc[s] = psum.tile([P, N], F32, name="acc")
+            for z in range(2):
+                cols = slice((2 * half + z) * P, (2 * half + z + 1) * P)
+                w_cols = slice(z * N, (z + 1) * N)
+                nc.tensor.matmul_mx(
+                    out=acc[s][:],
+                    lhsT=dz_codes[q][:, cols].bitcast(E5M2X4),
+                    lhsT_scale=dz_scales[q][:, cols],
+                    rhs=w_codes[:, w_cols].bitcast(E4M3X4),
+                    rhs_scale=w_scales[:, w_cols],
+                    start=(z == 0),
+                    stop=(z == 1),
+                )
 
-        def store_pair(q):
-            out_sb = results.tile([P, 2, N], F32, name="out_sb")
-            for half in range(2):
-                nc.scalar.mul(out=out_sb[:, half, :], in_=acc[2 * q + half][:], mul=-1.0)
-            nc.sync.dma_start(out=out_rows[:, 2 * q : 2 * q + 2, :], in_=out_sb[:])
+        def store(s, on_vector):
+            out_sb = results.tile([P, N], F32, name="out_sb")
+            if on_vector:
+                nc.vector.tensor_scalar_mul(out=out_sb[:], in0=acc[s][:], scalar1=-1.0)
+            else:
+                nc.scalar.mul(out=out_sb[:], in_=acc[s][:], mul=-1.0)
+            nc.sync.dma_start(out=out_rows[:, s, :], in_=out_sb[:])
 
-        gate_product(0)
-        gate_product(1)
-        transpose_slot(0)
-        scalar_parts(0)
-        quantised = 0
-        multiplied = 0
-        stored = 0
+        for s in range(3):
+            gate_product(s)
+        for s in range(2):
+            transpose_y(s)
+            scalar_parts(s)
+            transpose_o(s)
+            transpose_go(s)
         for s in range(SLOTS):
+            if s + 3 < SLOTS:
+                gate_product(s + 3)
             if s + 2 < SLOTS:
-                gate_product(s + 2)
-            if s + 1 < SLOTS:
-                transpose_slot(s + 1)
-                scalar_parts(s + 1)
-            if FIRST_W_STEP <= s < FIRST_W_STEP + W_PIECES:
-                transpose_weight_piece(s - FIRST_W_STEP)
-            if stored < multiplied:
-                store_pair(stored)
-                stored += 1
-            gradients(s)
-            if s == FIRST_W_STEP + W_PIECES:
-                quantise_weights()
+                transpose_y(s + 2)
+                scalar_parts(s + 2)
+            gate_factor(s)
+            if s + 2 < SLOTS:
+                transpose_o(s + 2)
             if s >= 2 and s % 2 == 0:
-                quantise_pair(quantised)
-                quantised += 1
-            if s >= FIRST_PRODUCT_STEP and multiplied < quantised:
-                multiply_pair(multiplied)
-                multiplied += 1
-        quantise_pair(quantised)
-        quantised += 1
-        while stored < PAIRS:
-            if multiplied < PAIRS:
-                multiply_pair(multiplied)
-                multiplied += 1
-            store_pair(stored)
-            stored += 1
+                quantise_pair(s // 2 - 1)
+            if s >= 2:
+                multiply(s - 2)
+            gradients(s)
+            if s + 2 < SLOTS:
+                transpose_go(s + 2)
+            if s >= 2:
+                store(s - 2, False)
+        quantise_pair(PAIRS - 1)
+        multiply(SLOTS - 2)
+        multiply(SLOTS - 1)
+        store(SLOTS - 2, False)
+        store(SLOTS - 1, True)

@@ -19,6 +19,7 @@ K = P * PACK
 N = 512
 SLOTS = B // P
 PAIRS = SLOTS // 2
+WARM_UP = 5
 
 FLOPS = 2 * 2 * B * K * N
 BYTES = B * K * (2 + 4 + 4) + 2 * N * K * 2 + B * N * 4
@@ -39,6 +40,12 @@ def tile_gatel0rdcell_pb_v_kernel(tc, x_t, h_t, Wy, by, Wo, bo, y_hat, o_t, grad
         results = stack.enter_context(tc.tile_pool(name="results", bufs=SLOTS))
         psum = stack.enter_context(tc.psum_pool(name="psum", bufs=2))
         stack.enter_context(tc.manual_schedule())
+
+        zeros = const.tile([P, N], BF16, name="zeros")
+        nc.vector.memset(zeros[:], 0.0)
+        warm_ps = psum.tile([P, N], F32, name="warm_ps", tag="acc", bufs=1)
+        for i in range(WARM_UP):
+            nc.tensor.matmul(out=warm_ps[:], lhsT=zeros[:, 0:P], rhs=zeros[:], start=True, stop=True)
 
         ident_bf16 = const.tile([P, P], BF16, name="ident_bf16")
         make_identity(nc, ident_bf16[:])
@@ -115,7 +122,7 @@ def tile_gatel0rdcell_pb_v_kernel(tc, x_t, h_t, Wy, by, Wo, bo, y_hat, o_t, grad
             transpose_to(o_t_ps[s], o_in[s])
 
         def transpose_go(s):
-            go_t[s] = psum.tile([P, PACK, P], F32, name="go_t")
+            go_t[s] = psum.tile([P, PACK, P], F32, name="go_t", bufs=3)
             transpose_to(go_t[s], go_nat[s])
 
         def scalar_parts(s):
@@ -143,18 +150,21 @@ def tile_gatel0rdcell_pb_v_kernel(tc, x_t, h_t, Wy, by, Wo, bo, y_hat, o_t, grad
             )
             nc.vector.tensor_tensor(out=grouped[q][:, half, 1], in0=yo[s][:], in1=go_view, op=ALU.mult)
 
-        def quantise_pair(q):
-            dz_codes[q] = codes_pool.tile([P, 4 * P], U32, name="dz_codes", align_bytes=64)
-            dz_scales[q] = codes_pool.tile([P, 4 * P], U8, name="dz_scales", align_bytes=64)
+        def quantise(first, count):
+            q, half = divmod(first, 2)
+            if half == 0:
+                dz_codes[q] = codes_pool.tile([P, 4 * P], U32, name="dz_codes", align_bytes=64)
+                dz_scales[q] = codes_pool.tile([P, 4 * P], U8, name="dz_scales", align_bytes=64)
+            cols = slice(half * 2 * P, (half + count) * 2 * P)
             nc.vector.quantize_mx(
-                out=dz_codes[q][:].bitcast(E5M2X4),
-                scales=dz_scales[q][:],
-                in_=grouped[q][:].rearrange("p h z b t -> p (h z b t)"),
+                out=dz_codes[q][:, cols].bitcast(E5M2X4),
+                scales=dz_scales[q][:, cols],
+                in_=grouped[q][:, half : half + count].rearrange("p h z b t -> p (h z b t)"),
             )
 
         def multiply(s):
             q, half = divmod(s, 2)
-            acc[s] = psum.tile([P, N], F32, name="acc")
+            acc[s] = psum.tile([P, N], F32, name="acc", bufs=1)
             for z in range(2):
                 cols = slice((2 * half + z) * P, (2 * half + z + 1) * P)
                 w_cols = slice(z * N, (z + 1) * N)
@@ -181,28 +191,29 @@ def tile_gatel0rdcell_pb_v_kernel(tc, x_t, h_t, Wy, by, Wo, bo, y_hat, o_t, grad
         for s in range(2):
             transpose_y(s)
             scalar_parts(s)
-            transpose_o(s)
             transpose_go(s)
+            transpose_o(s)
         for s in range(SLOTS):
             if s + 3 < SLOTS:
                 gate_product(s + 3)
             if s + 2 < SLOTS:
                 transpose_y(s + 2)
                 scalar_parts(s + 2)
+                transpose_go(s + 2)
             gate_factor(s)
             if s + 2 < SLOTS:
                 transpose_o(s + 2)
             if s >= 2 and s % 2 == 0:
-                quantise_pair(s // 2 - 1)
+                quantise(s - 2, 2)
+            if s == SLOTS - 1:
+                quantise(s - 1, 1)
             if s >= 2:
                 multiply(s - 2)
             gradients(s)
-            if s + 2 < SLOTS:
-                transpose_go(s + 2)
             if s >= 2:
                 store(s - 2, False)
-        quantise_pair(PAIRS - 1)
         multiply(SLOTS - 2)
-        multiply(SLOTS - 1)
         store(SLOTS - 2, False)
+        quantise(SLOTS - 1, 1)
+        multiply(SLOTS - 1)
         store(SLOTS - 1, True)

@@ -18,7 +18,7 @@ B = 2048
 K = P * PACK
 N = 512
 SLOTS = B // P
-PAIRS = SLOTS // 2
+GROUP = 4
 WARM_UP = 5
 
 FLOPS = 2 * 2 * B * K * N
@@ -140,33 +140,33 @@ def tile_gatel0rdcell_pb_v_kernel(tc, x_t, h_t, Wy, by, Wo, bo, y_hat, o_t, grad
             )
 
         def gradients(s):
-            q, half = divmod(s, 2)
-            if half == 0:
-                grouped[q] = work.tile([P, 2, 2, P, PACK], BF16, name="grouped", align_bytes=64)
+            q, pos = divmod(s, GROUP)
+            if pos == 0:
+                grouped[q] = work.tile([P, GROUP, 2, P, PACK], BF16, name="grouped", align_bytes=64)
             go_view = go_t[s][:].rearrange("p t b -> p b t")
             nc.vector.scalar_tensor_tensor(
-                out=grouped[q][:, half, 0], in0=ysq_sb[s][:], scalar=1.0, in1=go_view,
+                out=grouped[q][:, pos, 0], in0=ysq_sb[s][:], scalar=1.0, in1=go_view,
                 op0=ALU.subtract, op1=ALU.mult,
             )
-            nc.vector.tensor_tensor(out=grouped[q][:, half, 1], in0=yo[s][:], in1=go_view, op=ALU.mult)
+            nc.vector.tensor_tensor(out=grouped[q][:, pos, 1], in0=yo[s][:], in1=go_view, op=ALU.mult)
 
         def quantise(first, count):
-            q, half = divmod(first, 2)
-            if half == 0:
-                dz_codes[q] = codes_pool.tile([P, 4 * P], U32, name="dz_codes", align_bytes=64)
-                dz_scales[q] = codes_pool.tile([P, 4 * P], U8, name="dz_scales", align_bytes=64)
-            cols = slice(half * 2 * P, (half + count) * 2 * P)
+            q, pos = divmod(first, GROUP)
+            if pos == 0:
+                dz_codes[q] = codes_pool.tile([P, GROUP * 2 * P], U32, name="dz_codes", align_bytes=64)
+                dz_scales[q] = codes_pool.tile([P, GROUP * 2 * P], U8, name="dz_scales", align_bytes=64)
+            cols = slice(pos * 2 * P, (pos + count) * 2 * P)
             nc.vector.quantize_mx(
                 out=dz_codes[q][:, cols].bitcast(E5M2X4),
                 scales=dz_scales[q][:, cols],
-                in_=grouped[q][:, half : half + count].rearrange("p h z b t -> p (h z b t)"),
+                in_=grouped[q][:, pos : pos + count].rearrange("p h z b t -> p (h z b t)"),
             )
 
         def multiply(s):
-            q, half = divmod(s, 2)
+            q, pos = divmod(s, GROUP)
             acc[s] = psum.tile([P, N], F32, name="acc", bufs=1)
             for z in range(2):
-                cols = slice((2 * half + z) * P, (2 * half + z + 1) * P)
+                cols = slice((2 * pos + z) * P, (2 * pos + z + 1) * P)
                 w_cols = slice(z * N, (z + 1) * N)
                 nc.tensor.matmul_mx(
                     out=acc[s][:],
@@ -203,17 +203,20 @@ def tile_gatel0rdcell_pb_v_kernel(tc, x_t, h_t, Wy, by, Wo, bo, y_hat, o_t, grad
             gate_factor(s)
             if s + 2 < SLOTS:
                 transpose_o(s + 2)
-            if s >= 2 and s % 2 == 0:
-                quantise(s - 2, 2)
+            if s >= GROUP and s % GROUP == 0:
+                quantise(s - GROUP, GROUP)
+            if s == SLOTS - 2:
+                quantise(SLOTS - GROUP, 2)
             if s == SLOTS - 1:
-                quantise(s - 1, 1)
-            if s >= 2:
-                multiply(s - 2)
+                quantise(SLOTS - 2, 1)
+            if s >= GROUP:
+                multiply(s - GROUP)
             gradients(s)
-            if s >= 2:
-                store(s - 2, False)
-        multiply(SLOTS - 2)
-        store(SLOTS - 2, False)
+            if s >= GROUP:
+                store(s - GROUP, False)
+        for s in range(SLOTS - GROUP, SLOTS - 1):
+            multiply(s)
+            store(s, False)
         quantise(SLOTS - 1, 1)
         multiply(SLOTS - 1)
         store(SLOTS - 1, True)

@@ -18,7 +18,6 @@ B = 2048
 K = P * PACK
 N = 512
 SLOTS = B // P
-GROUP = 4
 WARM_UP = 5
 
 FLOPS = 2 * 2 * B * K * N
@@ -35,7 +34,7 @@ def tile_gatel0rdcell_pb_v_kernel(tc, x_t, h_t, Wy, by, Wo, bo, y_hat, o_t, grad
     with ExitStack() as stack:
         const = stack.enter_context(tc.tile_pool(name="const", bufs=1))
         inputs = stack.enter_context(tc.tile_pool(name="inputs", bufs=1))
-        work = stack.enter_context(tc.tile_pool(name="work", bufs=3))
+        work = stack.enter_context(tc.tile_pool(name="work", bufs=4))
         codes_pool = stack.enter_context(tc.tile_pool(name="codes", bufs=3))
         results = stack.enter_context(tc.tile_pool(name="results", bufs=SLOTS))
         psum = stack.enter_context(tc.psum_pool(name="psum", bufs=2))
@@ -43,30 +42,24 @@ def tile_gatel0rdcell_pb_v_kernel(tc, x_t, h_t, Wy, by, Wo, bo, y_hat, o_t, grad
 
         zeros = const.tile([P, N], BF16, name="zeros")
         nc.vector.memset(zeros[:], 0.0)
-        warm_ps = psum.tile([P, N], F32, name="warm_ps", tag="acc", bufs=1)
+        warm_ps = psum.tile([P, N], F32, name="warm_ps", tag="acc")
         for i in range(WARM_UP):
             nc.tensor.matmul(out=warm_ps[:], lhsT=zeros[:, 0:P], rhs=zeros[:], start=True, stop=True)
 
-        ident_bf16 = const.tile([P, P], BF16, name="ident_bf16")
-        make_identity(nc, ident_bf16[:])
         ident_f32 = const.tile([P, P], F32, name="ident_f32")
         make_identity(nc, ident_f32[:])
-
-        w_raw = []
-        for name, w in (("wy_raw", Wy), ("wo_raw", Wo)):
-            raw = const.tile([P, N // P, K], BF16, name=name)
-            nc.sync.dma_start(out=raw[:], in_=w[0:N, :].rearrange("(c i) k -> i c k", i=P))
-            w_raw.append(raw)
+        ident_bf16 = const.tile([P, P], BF16, name="ident_bf16")
+        make_identity(nc, ident_bf16[:])
 
         y_in, o_in, g_in = {}, {}, {}
 
         def load_slots(first, count):
+            y_tile = inputs.tile([P, count, K], F32, name="y%d" % first)
             g_tile = inputs.tile([P, count, K], BF16, name="g%d" % first)
             o_tile = inputs.tile([P, count, K], F32, name="o%d" % first)
-            y_tile = inputs.tile([P, count, K], F32, name="y%d" % first)
+            nc.sync.dma_start(out=y_tile[:], in_=y_rows[:, first : first + count, :])
             nc.sync.dma_start(out=g_tile[:], in_=g_rows[:, first : first + count, :])
             nc.sync.dma_start(out=o_tile[:], in_=o_rows[:, first : first + count, :])
-            nc.sync.dma_start(out=y_tile[:], in_=y_rows[:, first : first + count, :])
             for j in range(count):
                 g_in[first + j] = g_tile[:, j, :]
                 o_in[first + j] = o_tile[:, j, :]
@@ -74,99 +67,107 @@ def tile_gatel0rdcell_pb_v_kernel(tc, x_t, h_t, Wy, by, Wo, bo, y_hat, o_t, grad
 
         load_slots(0, 1)
         load_slots(1, 1)
+        w_raw = []
+        for name, w in (("wy_raw", Wy), ("wo_raw", Wo)):
+            raw = const.tile([P, N // P, K], BF16, name=name)
+            nc.sync.dma_start(out=raw[:], in_=w[0:N, :].rearrange("(c i) k -> i c k", i=P))
+            w_raw.append(raw)
         for first in range(2, SLOTS, 2):
             load_slots(first, 2)
 
         w_grouped = const.tile([P, 2, N // P, P, PACK], BF16, name="w_grouped", align_bytes=64)
         w_codes = const.tile([P, 2 * N], U32, name="w_codes", align_bytes=64)
         w_scales = const.tile([P, 2 * N], U8, name="w_scales", align_bytes=64)
-        for z in range(2):
-            for part in range(2):
-                w_t = psum.tile([P, 2, PACK, P], BF16, name="w_t", tag=("y_t", "o_t_ps")[z])
-                for h in range(2):
-                    for t in range(PACK):
-                        nc.tensor.transpose(
-                            out=w_t[:, h, t, :],
-                            in_=w_raw[z][:, 2 * part + h, t * P : (t + 1) * P],
-                            identity=ident_bf16[:],
-                        )
-                dst = w_grouped[:, z, 2 * part : 2 * part + 2]
-                src = w_t[:].rearrange("p h t i -> p h i t")
-                if part == 0:
-                    nc.scalar.copy(out=dst, in_=src)
-                else:
-                    nc.vector.tensor_copy(out=dst, in_=src)
-        nc.vector.quantize_mx(
-            out=w_codes[:].bitcast(E4M3X4),
-            scales=w_scales[:],
-            in_=w_grouped[:].rearrange("p z c i t -> p (z c i t)"),
-        )
 
-        go_nat, y_t, o_t_ps, go_t, y_sb, ysq_sb, yo = {}, {}, {}, {}, {}, {}, {}
+        def transpose_weights():
+            for z in range(2):
+                for part in range(2):
+                    w_t = psum.tile([P, 2, PACK, P], BF16, name="w_t", tag="acc")
+                    for h in range(2):
+                        for t in range(PACK):
+                            nc.tensor.transpose(
+                                out=w_t[:, h, t, :],
+                                in_=w_raw[z][:, 2 * part + h, t * P : (t + 1) * P],
+                                identity=ident_bf16[:],
+                            )
+                    nc.scalar.copy(
+                        out=w_grouped[:, z, 2 * part : 2 * part + 2], in_=w_t[:].rearrange("p h t i -> p h i t")
+                    )
+
+        def quantise_weights():
+            nc.vector.quantize_mx(
+                out=w_codes[:].bitcast(E4M3X4),
+                scales=w_scales[:],
+                in_=w_grouped[:].rearrange("p z c i t -> p (z c i t)"),
+            )
+
+        ysq, gy, u, o_ps, u_ps, gy_ps, o_sb, w_fac = {}, {}, {}, {}, {}, {}, {}, {}
         grouped, dz_codes, dz_scales, acc = {}, {}, {}, {}
+
+        def by_word(ps):
+            return ps[:].rearrange("p t b -> p b t")
 
         def transpose_to(dst, src):
             for t in range(PACK):
                 nc.tensor.transpose(out=dst[:, t, :], in_=src[:, t * P : (t + 1) * P], identity=ident_f32[:])
 
-        def gate_product(s):
-            go_nat[s] = work.tile([P, K], F32, name="go_nat", bufs=4)
-            nc.gpsimd.tensor_tensor(out=go_nat[s][:], in0=g_in[s], in1=o_in[s], op=ALU.mult)
+        def natural(s):
+            ysq[s] = work.tile([P, K], F32, name="ysq")
+            nc.scalar.activation(out=ysq[s][:], in_=y_in[s], func=ACT.Square)
+            gy[s] = work.tile([P, K], F32, name="gy")
+            nc.gpsimd.tensor_tensor(out=gy[s][:], in0=g_in[s], in1=y_in[s], op=ALU.mult)
+            u[s] = work.tile([P, K], F32, name="u")
+            if s % 2 == 1:
+                m = work.tile([P, K], F32, name="m")
+                nc.scalar.activation(out=m[:], in_=ysq[s][:], func=ACT.Identity, bias=-1.0)
+                nc.gpsimd.tensor_tensor(out=u[s][:], in0=m[:], in1=g_in[s], op=ALU.mult)
 
-        def transpose_y(s):
-            y_t[s] = psum.tile([P, PACK, P], F32, name="y_t")
-            transpose_to(y_t[s], y_in[s])
+        def natural_on_vector(s):
+            if s % 2 == 0:
+                nc.vector.scalar_tensor_tensor(
+                    out=u[s][:], in0=ysq[s][:], scalar=1.0, in1=g_in[s], op0=ALU.subtract, op1=ALU.mult
+                )
 
-        def transpose_o(s):
-            o_t_ps[s] = psum.tile([P, PACK, P], F32, name="o_t_ps")
-            transpose_to(o_t_ps[s], o_in[s])
-
-        def transpose_go(s):
-            go_t[s] = psum.tile([P, PACK, P], F32, name="go_t", bufs=3)
-            transpose_to(go_t[s], go_nat[s])
-
-        def scalar_parts(s):
-            y_sb[s] = work.tile([P, P, PACK], F32, name="y_sb")
-            ysq_sb[s] = work.tile([P, P, PACK], F32, name="ysq_sb")
-            y_view = y_t[s][:].rearrange("p t b -> p b t")
-            nc.scalar.copy(out=y_sb[s][:], in_=y_view)
-            nc.scalar.activation(out=ysq_sb[s][:], in_=y_view, func=ACT.Square)
+        def transposes(s):
+            o_ps[s] = psum.tile([P, PACK, P], F32, name="o_ps")
+            transpose_to(o_ps[s], o_in[s])
+            o_sb[s] = work.tile([P, P, PACK], F32, name="o_sb")
+            nc.scalar.copy(out=o_sb[s][:], in_=by_word(o_ps[s]))
+            u_ps[s] = psum.tile([P, PACK, P], F32, name="u_ps")
+            transpose_to(u_ps[s], u[s])
+            gy_ps[s] = psum.tile([P, PACK, P], F32, name="gy_ps")
+            transpose_to(gy_ps[s], gy[s])
 
         def gate_factor(s):
-            yo[s] = work.tile([P, P, PACK], F32, name="yo")
+            w_fac[s] = work.tile([P, P, PACK], F32, name="w_fac")
             nc.vector.scalar_tensor_tensor(
-                out=yo[s][:], in0=o_t_ps[s][:].rearrange("p t b -> p b t"), scalar=1.0, in1=y_sb[s][:],
-                op0=ALU.subtract, op1=ALU.mult,
+                out=w_fac[s][:], in0=by_word(o_ps[s]), scalar=1.0, in1=o_sb[s][:], op0=ALU.subtract, op1=ALU.mult
             )
 
         def gradients(s):
-            q, pos = divmod(s, GROUP)
-            if pos == 0:
-                grouped[q] = work.tile([P, GROUP, 2, P, PACK], BF16, name="grouped", align_bytes=64)
-            go_view = go_t[s][:].rearrange("p t b -> p b t")
-            nc.vector.scalar_tensor_tensor(
-                out=grouped[q][:, pos, 0], in0=ysq_sb[s][:], scalar=1.0, in1=go_view,
-                op0=ALU.subtract, op1=ALU.mult,
-            )
-            nc.vector.tensor_tensor(out=grouped[q][:, pos, 1], in0=yo[s][:], in1=go_view, op=ALU.mult)
+            q, half = divmod(s, 2)
+            if half == 0:
+                grouped[q] = work.tile([P, 2, 2, P, PACK], BF16, name="grouped", align_bytes=64)
+            nc.vector.tensor_tensor(out=grouped[q][:, half, 0], in0=by_word(u_ps[s]), in1=o_sb[s][:], op=ALU.mult)
+            nc.vector.tensor_tensor(out=grouped[q][:, half, 1], in0=by_word(gy_ps[s]), in1=w_fac[s][:], op=ALU.mult)
 
         def quantise(first, count):
-            q, pos = divmod(first, GROUP)
-            if pos == 0:
-                dz_codes[q] = codes_pool.tile([P, GROUP * 2 * P], U32, name="dz_codes", align_bytes=64)
-                dz_scales[q] = codes_pool.tile([P, GROUP * 2 * P], U8, name="dz_scales", align_bytes=64)
-            cols = slice(pos * 2 * P, (pos + count) * 2 * P)
+            q, half = divmod(first, 2)
+            if half == 0:
+                dz_codes[q] = codes_pool.tile([P, 4 * P], U32, name="dz_codes", align_bytes=64)
+                dz_scales[q] = codes_pool.tile([P, 4 * P], U8, name="dz_scales", align_bytes=64)
+            cols = slice(half * 2 * P, (half + count) * 2 * P)
             nc.vector.quantize_mx(
                 out=dz_codes[q][:, cols].bitcast(E5M2X4),
                 scales=dz_scales[q][:, cols],
-                in_=grouped[q][:, pos : pos + count].rearrange("p h z b t -> p (h z b t)"),
+                in_=grouped[q][:, half : half + count].rearrange("p h z b t -> p (h z b t)"),
             )
 
         def multiply(s):
-            q, pos = divmod(s, GROUP)
-            acc[s] = psum.tile([P, N], F32, name="acc", bufs=1)
+            q, half = divmod(s, 2)
+            acc[s] = psum.tile([P, N], F32, name="acc")
             for z in range(2):
-                cols = slice((2 * pos + z) * P, (2 * pos + z + 1) * P)
+                cols = slice((2 * half + z) * P, (2 * half + z + 1) * P)
                 w_cols = slice(z * N, (z + 1) * N)
                 nc.tensor.matmul_mx(
                     out=acc[s][:],
@@ -186,37 +187,35 @@ def tile_gatel0rdcell_pb_v_kernel(tc, x_t, h_t, Wy, by, Wo, bo, y_hat, o_t, grad
                 nc.scalar.mul(out=out_sb[:], in_=acc[s][:], mul=-1.0)
             nc.sync.dma_start(out=out_rows[:, s, :], in_=out_sb[:])
 
-        for s in range(3):
-            gate_product(s)
-        for s in range(2):
-            transpose_y(s)
-            scalar_parts(s)
-            transpose_go(s)
-            transpose_o(s)
+        natural(0)
+        natural_on_vector(0)
+        transposes(0)
+        natural(1)
+        transposes(1)
+        natural(2)
+        transpose_weights()
         for s in range(SLOTS):
             if s + 3 < SLOTS:
-                gate_product(s + 3)
-            if s + 2 < SLOTS:
-                transpose_y(s + 2)
-                scalar_parts(s + 2)
-                transpose_go(s + 2)
+                natural(s + 3)
             gate_factor(s)
-            if s + 2 < SLOTS:
-                transpose_o(s + 2)
-            if s >= GROUP and s % GROUP == 0:
-                quantise(s - GROUP, GROUP)
-            if s == SLOTS - 2:
-                quantise(SLOTS - GROUP, 2)
+            if s >= 2 and s % 2 == 0:
+                quantise(s - 2, 2)
             if s == SLOTS - 1:
-                quantise(SLOTS - 2, 1)
-            if s >= GROUP:
-                multiply(s - GROUP)
+                quantise(s - 1, 1)
             gradients(s)
-            if s >= GROUP:
-                store(s - GROUP, False)
-        for s in range(SLOTS - GROUP, SLOTS - 1):
-            multiply(s)
-            store(s, False)
+            if s == 0:
+                natural_on_vector(2)
+            if s == 1:
+                quantise_weights()
+            if s + 3 < SLOTS:
+                natural_on_vector(s + 3)
+            if s + 2 < SLOTS:
+                transposes(s + 2)
+            if s >= 2:
+                multiply(s - 2)
+                store(s - 2, False)
+        multiply(SLOTS - 2)
+        store(SLOTS - 2, False)
         quantise(SLOTS - 1, 1)
         multiply(SLOTS - 1)
         store(SLOTS - 1, True)

@@ -34,7 +34,7 @@ def tile_gatel0rdcell_pb_v_kernel(tc, x_t, h_t, Wy, by, Wo, bo, y_hat, o_t, grad
     with ExitStack() as stack:
         const = stack.enter_context(tc.tile_pool(name="const", bufs=1))
         inputs = stack.enter_context(tc.tile_pool(name="inputs", bufs=1))
-        work = stack.enter_context(tc.tile_pool(name="work", bufs=4))
+        work = stack.enter_context(tc.tile_pool(name="work", bufs=3))
         codes_pool = stack.enter_context(tc.tile_pool(name="codes", bufs=3))
         results = stack.enter_context(tc.tile_pool(name="results", bufs=SLOTS))
         psum = stack.enter_context(tc.psum_pool(name="psum", bufs=2))
@@ -42,7 +42,7 @@ def tile_gatel0rdcell_pb_v_kernel(tc, x_t, h_t, Wy, by, Wo, bo, y_hat, o_t, grad
 
         zeros = const.tile([P, N], BF16, name="zeros")
         nc.vector.memset(zeros[:], 0.0)
-        warm_ps = psum.tile([P, N], F32, name="warm_ps", tag="acc")
+        warm_ps = psum.tile([P, N], F32, name="warm_ps", tag="acc", bufs=1)
         for i in range(WARM_UP):
             nc.tensor.matmul(out=warm_ps[:], lhsT=zeros[:, 0:P], rhs=zeros[:], start=True, stop=True)
 
@@ -66,12 +66,12 @@ def tile_gatel0rdcell_pb_v_kernel(tc, x_t, h_t, Wy, by, Wo, bo, y_hat, o_t, grad
                 y_in[first + j] = y_tile[:, j, :]
 
         load_slots(0, 1)
-        load_slots(1, 1)
         w_raw = []
         for name, w in (("wy_raw", Wy), ("wo_raw", Wo)):
             raw = const.tile([P, N // P, K], BF16, name=name)
             nc.sync.dma_start(out=raw[:], in_=w[0:N, :].rearrange("(c i) k -> i c k", i=P))
             w_raw.append(raw)
+        load_slots(1, 1)
         for first in range(2, SLOTS, 2):
             load_slots(first, 2)
 
@@ -82,7 +82,7 @@ def tile_gatel0rdcell_pb_v_kernel(tc, x_t, h_t, Wy, by, Wo, bo, y_hat, o_t, grad
         def transpose_weights():
             for z in range(2):
                 for part in range(2):
-                    w_t = psum.tile([P, 2, PACK, P], BF16, name="w_t", tag="acc")
+                    w_t = psum.tile([P, 2, PACK, P], BF16, name="w_t", tag=("o_ps", "yu_ps", "gy_ps", "acc")[2 * z + part], bufs=(2, 2, 2, 1)[2 * z + part])
                     for h in range(2):
                         for t in range(PACK):
                             nc.tensor.transpose(
@@ -101,7 +101,7 @@ def tile_gatel0rdcell_pb_v_kernel(tc, x_t, h_t, Wy, by, Wo, bo, y_hat, o_t, grad
                 in_=w_grouped[:].rearrange("p z c i t -> p (z c i t)"),
             )
 
-        ysq, gy, u, o_ps, u_ps, gy_ps, o_sb, w_fac = {}, {}, {}, {}, {}, {}, {}, {}
+        gy, u, ysq_t, u_t, g_ps, o_ps, u_ps, gy_ps, o_sb, w_fac = {}, {}, {}, {}, {}, {}, {}, {}, {}, {}
         grouped, dz_codes, dz_scales, acc = {}, {}, {}, {}
 
         def by_word(ps):
@@ -111,34 +111,47 @@ def tile_gatel0rdcell_pb_v_kernel(tc, x_t, h_t, Wy, by, Wo, bo, y_hat, o_t, grad
             for t in range(PACK):
                 nc.tensor.transpose(out=dst[:, t, :], in_=src[:, t * P : (t + 1) * P], identity=ident_f32[:])
 
+        def on_vector(s):
+            return s % 2 == 0
+
         def natural(s):
-            ysq[s] = work.tile([P, K], F32, name="ysq")
-            nc.scalar.activation(out=ysq[s][:], in_=y_in[s], func=ACT.Square)
-            gy[s] = work.tile([P, K], F32, name="gy")
+            gy[s] = work.tile([P, K], F32, name="gy", bufs=7)
             nc.gpsimd.tensor_tensor(out=gy[s][:], in0=g_in[s], in1=y_in[s], op=ALU.mult)
-            u[s] = work.tile([P, K], F32, name="u")
-            if s % 2 == 1:
+            if not on_vector(s):
+                ysq = work.tile([P, K], F32, name="ysq")
+                nc.scalar.activation(out=ysq[:], in_=y_in[s], func=ACT.Square)
                 m = work.tile([P, K], F32, name="m")
-                nc.scalar.activation(out=m[:], in_=ysq[s][:], func=ACT.Identity, bias=-1.0)
+                nc.scalar.activation(out=m[:], in_=ysq[:], func=ACT.Identity, bias=-1.0)
+                u[s] = work.tile([P, K], F32, name="u")
                 nc.gpsimd.tensor_tensor(out=u[s][:], in0=m[:], in1=g_in[s], op=ALU.mult)
 
-        def natural_on_vector(s):
-            if s % 2 == 0:
-                nc.vector.scalar_tensor_tensor(
-                    out=u[s][:], in0=ysq[s][:], scalar=1.0, in1=g_in[s], op0=ALU.subtract, op1=ALU.mult
-                )
-
         def transposes(s):
+            if on_vector(s):
+                y_ps = psum.tile([P, PACK, P], F32, name="y_ps", tag="yu_ps")
+                transpose_to(y_ps, y_in[s])
+                ysq_t[s] = work.tile([P, P, PACK], F32, name="ysq_t")
+                nc.scalar.activation(out=ysq_t[s][:], in_=by_word(y_ps), func=ACT.Square)
+                g_ps[s] = psum.tile([P, PACK, P], BF16, name="g_ps", bufs=1)
+                for t in range(PACK):
+                    nc.tensor.transpose(
+                        out=g_ps[s][:, t, :], in_=g_in[s][:, t * P : (t + 1) * P], identity=ident_bf16[:]
+                    )
             o_ps[s] = psum.tile([P, PACK, P], F32, name="o_ps")
             transpose_to(o_ps[s], o_in[s])
             o_sb[s] = work.tile([P, P, PACK], F32, name="o_sb")
             nc.scalar.copy(out=o_sb[s][:], in_=by_word(o_ps[s]))
-            u_ps[s] = psum.tile([P, PACK, P], F32, name="u_ps")
-            transpose_to(u_ps[s], u[s])
+            if not on_vector(s):
+                u_ps[s] = psum.tile([P, PACK, P], F32, name="u_ps", tag="yu_ps")
+                transpose_to(u_ps[s], u[s])
             gy_ps[s] = psum.tile([P, PACK, P], F32, name="gy_ps")
             transpose_to(gy_ps[s], gy[s])
 
-        def gate_factor(s):
+        def factors(s):
+            if on_vector(s):
+                u_t[s] = work.tile([P, P, PACK], F32, name="u_t")
+                nc.vector.scalar_tensor_tensor(
+                    out=u_t[s][:], in0=ysq_t[s][:], scalar=1.0, in1=by_word(g_ps[s]), op0=ALU.subtract, op1=ALU.mult
+                )
             w_fac[s] = work.tile([P, P, PACK], F32, name="w_fac")
             nc.vector.scalar_tensor_tensor(
                 out=w_fac[s][:], in0=by_word(o_ps[s]), scalar=1.0, in1=o_sb[s][:], op0=ALU.subtract, op1=ALU.mult
@@ -148,7 +161,11 @@ def tile_gatel0rdcell_pb_v_kernel(tc, x_t, h_t, Wy, by, Wo, bo, y_hat, o_t, grad
             q, half = divmod(s, 2)
             if half == 0:
                 grouped[q] = work.tile([P, 2, 2, P, PACK], BF16, name="grouped", align_bytes=64)
-            nc.vector.tensor_tensor(out=grouped[q][:, half, 0], in0=by_word(u_ps[s]), in1=o_sb[s][:], op=ALU.mult)
+            if on_vector(s):
+                in0, in1 = by_word(o_ps[s]), u_t[s][:]
+            else:
+                in0, in1 = by_word(u_ps[s]), o_sb[s][:]
+            nc.vector.tensor_tensor(out=grouped[q][:, half, 0], in0=in0, in1=in1, op=ALU.mult)
             nc.vector.tensor_tensor(out=grouped[q][:, half, 1], in0=by_word(gy_ps[s]), in1=w_fac[s][:], op=ALU.mult)
 
         def quantise(first, count):
@@ -165,7 +182,7 @@ def tile_gatel0rdcell_pb_v_kernel(tc, x_t, h_t, Wy, by, Wo, bo, y_hat, o_t, grad
 
         def multiply(s):
             q, half = divmod(s, 2)
-            acc[s] = psum.tile([P, N], F32, name="acc")
+            acc[s] = psum.tile([P, N], F32, name="acc", bufs=1)
             for z in range(2):
                 cols = slice((2 * half + z) * P, (2 * half + z + 1) * P)
                 w_cols = slice(z * N, (z + 1) * N)
@@ -187,28 +204,29 @@ def tile_gatel0rdcell_pb_v_kernel(tc, x_t, h_t, Wy, by, Wo, bo, y_hat, o_t, grad
                 nc.scalar.mul(out=out_sb[:], in_=acc[s][:], mul=-1.0)
             nc.sync.dma_start(out=out_rows[:, s, :], in_=out_sb[:])
 
+        def ahead(i):
+            return min(i + 4, 2 + i + (i + 1) // 2, SLOTS - 1)
+
         natural(0)
-        natural_on_vector(0)
         transposes(0)
+        factors(0)
+        gradients(0)
+        transpose_weights()
         natural(1)
         transposes(1)
-        natural(2)
-        transpose_weights()
+        quantise_weights()
+        next_natural = 2
         for s in range(SLOTS):
-            if s + 3 < SLOTS:
-                natural(s + 3)
-            gate_factor(s)
-            if s >= 2 and s % 2 == 0:
-                quantise(s - 2, 2)
-            if s == SLOTS - 1:
-                quantise(s - 1, 1)
-            gradients(s)
-            if s == 0:
-                natural_on_vector(2)
-            if s == 1:
-                quantise_weights()
-            if s + 3 < SLOTS:
-                natural_on_vector(s + 3)
+            if s >= 1:
+                factors(s)
+                if s >= 2 and s % 2 == 0:
+                    quantise(s - 2, 2)
+                if s == SLOTS - 1:
+                    quantise(s - 1, 1)
+                gradients(s)
+            while next_natural <= ahead(s):
+                natural(next_natural)
+                next_natural += 1
             if s + 2 < SLOTS:
                 transposes(s + 2)
             if s >= 2:

@@ -35,14 +35,14 @@ def tile_gatel0rdcell_pb_v_kernel(tc, x_t, h_t, Wy, by, Wo, bo, y_hat, o_t, grad
         const = stack.enter_context(tc.tile_pool(name="const", bufs=1))
         inputs = stack.enter_context(tc.tile_pool(name="inputs", bufs=1))
         work = stack.enter_context(tc.tile_pool(name="work", bufs=3))
-        codes_pool = stack.enter_context(tc.tile_pool(name="codes", bufs=3))
+        codes_pool = stack.enter_context(tc.tile_pool(name="codes", bufs=5))
         results = stack.enter_context(tc.tile_pool(name="results", bufs=SLOTS))
         psum = stack.enter_context(tc.psum_pool(name="psum", bufs=2))
         stack.enter_context(tc.manual_schedule())
 
         zeros = const.tile([P, N], BF16, name="zeros")
         nc.vector.memset(zeros[:], 0.0)
-        warm_ps = psum.tile([P, N], F32, name="warm_ps", tag="acc", bufs=1)
+        warm_ps = psum.tile([P, N], F32, name="warm_ps", tag="acc", bufs=2)
         for i in range(WARM_UP):
             nc.tensor.matmul(out=warm_ps[:], lhsT=zeros[:, 0:P], rhs=zeros[:], start=True, stop=True)
 
@@ -65,34 +65,32 @@ def tile_gatel0rdcell_pb_v_kernel(tc, x_t, h_t, Wy, by, Wo, bo, y_hat, o_t, grad
                 o_in[first + j] = o_tile[:, j, :]
                 y_in[first + j] = y_tile[:, j, :]
 
-        load_slots(0, 1)
+        for s in range(4):
+            load_slots(s, 1)
         w_raw = []
         for name, w in (("wy_raw", Wy), ("wo_raw", Wo)):
             raw = const.tile([P, N // P, K], BF16, name=name)
             nc.sync.dma_start(out=raw[:], in_=w[0:N, :].rearrange("(c i) k -> i c k", i=P))
             w_raw.append(raw)
-        load_slots(1, 1)
-        for first in range(2, SLOTS, 2):
+        load_slots(4, 1)
+        load_slots(5, 1)
+        for first in range(6, SLOTS, 2):
             load_slots(first, 2)
 
         w_grouped = const.tile([P, 2, N // P, P, PACK], BF16, name="w_grouped", align_bytes=64)
         w_codes = const.tile([P, 2 * N], U32, name="w_codes", align_bytes=64)
         w_scales = const.tile([P, 2 * N], U8, name="w_scales", align_bytes=64)
 
-        def transpose_weights():
-            for z in range(2):
-                for part in range(2):
-                    w_t = psum.tile([P, 2, PACK, P], BF16, name="w_t", tag=("o_ps", "yu_ps", "gy_ps", "acc")[2 * z + part], bufs=(2, 2, 2, 1)[2 * z + part])
-                    for h in range(2):
-                        for t in range(PACK):
-                            nc.tensor.transpose(
-                                out=w_t[:, h, t, :],
-                                in_=w_raw[z][:, 2 * part + h, t * P : (t + 1) * P],
-                                identity=ident_bf16[:],
-                            )
-                    nc.scalar.copy(
-                        out=w_grouped[:, z, 2 * part : 2 * part + 2], in_=w_t[:].rearrange("p h t i -> p h i t")
+        def transpose_weights(z, part):
+            w_t = psum.tile([P, 2, PACK, P], BF16, name="w_t", tag="acc", bufs=2)
+            for h in range(2):
+                for t in range(PACK):
+                    nc.tensor.transpose(
+                        out=w_t[:, h, t, :],
+                        in_=w_raw[z][:, 2 * part + h, t * P : (t + 1) * P],
+                        identity=ident_bf16[:],
                     )
+            nc.scalar.copy(out=w_grouped[:, z, 2 * part : 2 * part + 2], in_=w_t[:].rearrange("p h t i -> p h i t"))
 
         def quantise_weights():
             nc.vector.quantize_mx(
@@ -101,7 +99,7 @@ def tile_gatel0rdcell_pb_v_kernel(tc, x_t, h_t, Wy, by, Wo, bo, y_hat, o_t, grad
                 in_=w_grouped[:].rearrange("p z c i t -> p (z c i t)"),
             )
 
-        gy, u, ysq_t, u_t, g_ps, o_ps, u_ps, gy_ps, o_sb, w_fac = {}, {}, {}, {}, {}, {}, {}, {}, {}, {}
+        go, goy, ysq, y_sb, goy_sb, u, yo, g_ps, o_ps, go_ps = {}, {}, {}, {}, {}, {}, {}, {}, {}, {}
         grouped, dz_codes, dz_scales, acc = {}, {}, {}, {}
 
         def by_word(ps):
@@ -112,61 +110,63 @@ def tile_gatel0rdcell_pb_v_kernel(tc, x_t, h_t, Wy, by, Wo, bo, y_hat, o_t, grad
                 nc.tensor.transpose(out=dst[:, t, :], in_=src[:, t * P : (t + 1) * P], identity=ident_f32[:])
 
         def on_vector(s):
-            return s % 2 == 0
+            return s < 10 or s % 2 == 0
 
         def natural(s):
-            gy[s] = work.tile([P, K], F32, name="gy", bufs=7)
-            nc.gpsimd.tensor_tensor(out=gy[s][:], in0=g_in[s], in1=y_in[s], op=ALU.mult)
+            go[s] = work.tile([P, K], F32, name="go", bufs=6)
+            nc.gpsimd.tensor_tensor(out=go[s][:], in0=g_in[s], in1=o_in[s], op=ALU.mult)
             if not on_vector(s):
-                ysq = work.tile([P, K], F32, name="ysq")
-                nc.scalar.activation(out=ysq[:], in_=y_in[s], func=ACT.Square)
-                m = work.tile([P, K], F32, name="m")
-                nc.scalar.activation(out=m[:], in_=ysq[:], func=ACT.Identity, bias=-1.0)
-                u[s] = work.tile([P, K], F32, name="u")
-                nc.gpsimd.tensor_tensor(out=u[s][:], in0=m[:], in1=g_in[s], op=ALU.mult)
+                goy[s] = work.tile([P, K], F32, name="goy", bufs=6)
+                nc.gpsimd.tensor_tensor(out=goy[s][:], in0=go[s][:], in1=y_in[s], op=ALU.mult)
 
-        def transposes(s):
+        def transpose_y(s):
+            y_ps = psum.tile([P, PACK, P], F32, name="y_ps", bufs=1)
+            transpose_to(y_ps, y_in[s])
+            ysq[s] = work.tile([P, P, PACK], F32, name="ysq")
+            nc.scalar.activation(out=ysq[s][:], in_=by_word(y_ps), func=ACT.Square)
             if on_vector(s):
-                y_ps = psum.tile([P, PACK, P], F32, name="y_ps", tag="yu_ps")
-                transpose_to(y_ps, y_in[s])
-                ysq_t[s] = work.tile([P, P, PACK], F32, name="ysq_t")
-                nc.scalar.activation(out=ysq_t[s][:], in_=by_word(y_ps), func=ACT.Square)
-                g_ps[s] = psum.tile([P, PACK, P], BF16, name="g_ps", bufs=1)
-                for t in range(PACK):
-                    nc.tensor.transpose(
-                        out=g_ps[s][:, t, :], in_=g_in[s][:, t * P : (t + 1) * P], identity=ident_bf16[:]
-                    )
+                y_sb[s] = work.tile([P, P, PACK], F32, name="y_sb")
+                nc.scalar.copy(out=y_sb[s][:], in_=by_word(y_ps))
+
+        def transpose_g(s):
+            g_ps[s] = psum.tile([P, PACK, P], BF16, name="g_ps", bufs=1)
+            for t in range(PACK):
+                nc.tensor.transpose(out=g_ps[s][:, t, :], in_=g_in[s][:, t * P : (t + 1) * P], identity=ident_bf16[:])
+
+        def transpose_o(s):
             o_ps[s] = psum.tile([P, PACK, P], F32, name="o_ps")
             transpose_to(o_ps[s], o_in[s])
-            o_sb[s] = work.tile([P, P, PACK], F32, name="o_sb")
-            nc.scalar.copy(out=o_sb[s][:], in_=by_word(o_ps[s]))
+
+        def transpose_go(s):
+            go_ps[s] = psum.tile([P, PACK, P], F32, name="go_ps")
+            transpose_to(go_ps[s], go[s] if on_vector(s) else goy[s])
             if not on_vector(s):
-                u_ps[s] = psum.tile([P, PACK, P], F32, name="u_ps", tag="yu_ps")
-                transpose_to(u_ps[s], u[s])
-            gy_ps[s] = psum.tile([P, PACK, P], F32, name="gy_ps")
-            transpose_to(gy_ps[s], gy[s])
+                goy_sb[s] = work.tile([P, P, PACK], F32, name="goy_sb")
+                nc.scalar.copy(out=goy_sb[s][:], in_=by_word(go_ps[s]))
 
         def factors(s):
-            if on_vector(s):
-                u_t[s] = work.tile([P, P, PACK], F32, name="u_t")
-                nc.vector.scalar_tensor_tensor(
-                    out=u_t[s][:], in0=ysq_t[s][:], scalar=1.0, in1=by_word(g_ps[s]), op0=ALU.subtract, op1=ALU.mult
-                )
-            w_fac[s] = work.tile([P, P, PACK], F32, name="w_fac")
+            u[s] = work.tile([P, P, PACK], F32, name="u")
             nc.vector.scalar_tensor_tensor(
-                out=w_fac[s][:], in0=by_word(o_ps[s]), scalar=1.0, in1=o_sb[s][:], op0=ALU.subtract, op1=ALU.mult
+                out=u[s][:], in0=ysq[s][:], scalar=1.0, in1=by_word(g_ps[s]), op0=ALU.subtract, op1=ALU.mult
             )
+            if on_vector(s):
+                yo[s] = work.tile([P, P, PACK], F32, name="yo")
+                nc.vector.scalar_tensor_tensor(
+                    out=yo[s][:], in0=by_word(o_ps[s]), scalar=1.0, in1=y_sb[s][:], op0=ALU.subtract, op1=ALU.mult
+                )
 
         def gradients(s):
             q, half = divmod(s, 2)
             if half == 0:
                 grouped[q] = work.tile([P, 2, 2, P, PACK], BF16, name="grouped", align_bytes=64)
+            if not on_vector(s):
+                nc.vector.scalar_tensor_tensor(
+                    out=grouped[q][:, half, 1], in0=by_word(o_ps[s]), scalar=1.0, in1=goy_sb[s][:],
+                    op0=ALU.subtract, op1=ALU.mult,
+                )
+            nc.vector.tensor_tensor(out=grouped[q][:, half, 0], in0=u[s][:], in1=by_word(o_ps[s]), op=ALU.mult)
             if on_vector(s):
-                in0, in1 = by_word(o_ps[s]), u_t[s][:]
-            else:
-                in0, in1 = by_word(u_ps[s]), o_sb[s][:]
-            nc.vector.tensor_tensor(out=grouped[q][:, half, 0], in0=in0, in1=in1, op=ALU.mult)
-            nc.vector.tensor_tensor(out=grouped[q][:, half, 1], in0=by_word(gy_ps[s]), in1=w_fac[s][:], op=ALU.mult)
+                nc.vector.tensor_tensor(out=grouped[q][:, half, 1], in0=yo[s][:], in1=by_word(go_ps[s]), op=ALU.mult)
 
         def quantise(first, count):
             q, half = divmod(first, 2)
@@ -182,7 +182,7 @@ def tile_gatel0rdcell_pb_v_kernel(tc, x_t, h_t, Wy, by, Wo, bo, y_hat, o_t, grad
 
         def multiply(s):
             q, half = divmod(s, 2)
-            acc[s] = psum.tile([P, N], F32, name="acc", bufs=1)
+            acc[s] = psum.tile([P, N], F32, name="acc", bufs=2)
             for z in range(2):
                 cols = slice((2 * half + z) * P, (2 * half + z + 1) * P)
                 w_cols = slice(z * N, (z + 1) * N)
@@ -204,36 +204,43 @@ def tile_gatel0rdcell_pb_v_kernel(tc, x_t, h_t, Wy, by, Wo, bo, y_hat, o_t, grad
                 nc.scalar.mul(out=out_sb[:], in_=acc[s][:], mul=-1.0)
             nc.sync.dma_start(out=out_rows[:, s, :], in_=out_sb[:])
 
-        def ahead(i):
-            return min(i + 4, 2 + i + (i + 1) // 2, SLOTS - 1)
-
         natural(0)
-        transposes(0)
-        factors(0)
-        gradients(0)
-        transpose_weights()
         natural(1)
-        transposes(1)
-        quantise_weights()
-        next_natural = 2
+        transpose_y(0)
+        natural(2)
+        transpose_o(0)
+        transpose_g(0)
+        transpose_y(1)
+        transpose_go(0)
         for s in range(SLOTS):
-            if s >= 1:
-                factors(s)
-                if s >= 2 and s % 2 == 0:
-                    quantise(s - 2, 2)
-                if s == SLOTS - 1:
-                    quantise(s - 1, 1)
-                gradients(s)
-            while next_natural <= ahead(s):
-                natural(next_natural)
-                next_natural += 1
+            factors(s)
+            if s >= 2 and s % 2 == 0:
+                quantise(s - 2, 2)
+            if s == SLOTS - 1:
+                quantise(s - 1, 1)
+            gradients(s)
+            if s == 3:
+                quantise_weights()
+            if s + 1 < SLOTS:
+                transpose_o(s + 1)
+                transpose_g(s + 1)
+            if s in (1, 2):
+                transpose_weights(s - 1, 0)
+                transpose_weights(s - 1, 1)
             if s + 2 < SLOTS:
-                transposes(s + 2)
-            if s >= 2:
-                multiply(s - 2)
-                store(s - 2, False)
+                transpose_y(s + 2)
+            if s + 1 < SLOTS:
+                transpose_go(s + 1)
+            if s >= 3:
+                multiply(s - 3)
+            if s + 3 < SLOTS:
+                natural(s + 3)
+            if s >= 3:
+                store(s - 3, False)
+        multiply(SLOTS - 3)
+        store(SLOTS - 3, False)
+        quantise(SLOTS - 1, 1)
         multiply(SLOTS - 2)
         store(SLOTS - 2, False)
-        quantise(SLOTS - 1, 1)
         multiply(SLOTS - 1)
         store(SLOTS - 1, True)

@@ -18,7 +18,7 @@ B = 2048
 K = P * PACK
 N = 512
 SLOTS = B // P
-WARM_UP = 5
+WARM_UP = 4
 
 FLOPS = 2 * 2 * B * K * N
 BYTES = B * K * (2 + 4 + 4) + 2 * N * K * 2 + B * N * 4
@@ -42,9 +42,13 @@ def tile_gatel0rdcell_pb_v_kernel(tc, x_t, h_t, Wy, by, Wo, bo, y_hat, o_t, grad
 
         zeros = const.tile([P, N], BF16, name="zeros")
         nc.vector.memset(zeros[:], 0.0)
-        warm_ps = psum.tile([P, N], F32, name="warm_ps", tag="acc", bufs=2)
-        for i in range(WARM_UP):
-            nc.tensor.matmul(out=warm_ps[:], lhsT=zeros[:, 0:P], rhs=zeros[:], start=True, stop=True)
+
+        def keep_warm(count):
+            warm_ps = psum.tile([P, N], F32, name="warm_ps", tag="acc", bufs=2)
+            for i in range(count):
+                nc.tensor.matmul(out=warm_ps[:], lhsT=zeros[:, 0:P], rhs=zeros[:], start=True, stop=True)
+
+        keep_warm(WARM_UP)
 
         ident_f32 = const.tile([P, P], F32, name="ident_f32")
         make_identity(nc, ident_f32[:])
@@ -110,7 +114,7 @@ def tile_gatel0rdcell_pb_v_kernel(tc, x_t, h_t, Wy, by, Wo, bo, y_hat, o_t, grad
                 nc.tensor.transpose(out=dst[:, t, :], in_=src[:, t * P : (t + 1) * P], identity=ident_f32[:])
 
         def on_vector(s):
-            return s < 10 or s % 2 == 0
+            return s < 8 or s % 2 == 0
 
         def natural(s):
             go[s] = work.tile([P, K], F32, name="go", bufs=6)
@@ -207,11 +211,14 @@ def tile_gatel0rdcell_pb_v_kernel(tc, x_t, h_t, Wy, by, Wo, bo, y_hat, o_t, grad
         natural(0)
         natural(1)
         transpose_y(0)
-        natural(2)
         transpose_o(0)
+        keep_warm(2)
         transpose_g(0)
-        transpose_y(1)
         transpose_go(0)
+        transpose_y(1)
+        natural(2)
+        multiplied = []
+        next_slot = 0
         for s in range(SLOTS):
             factors(s)
             if s >= 2 and s % 2 == 0:
@@ -221,24 +228,27 @@ def tile_gatel0rdcell_pb_v_kernel(tc, x_t, h_t, Wy, by, Wo, bo, y_hat, o_t, grad
             gradients(s)
             if s == 3:
                 quantise_weights()
+            for r in multiplied:
+                store(r, False)
             if s + 1 < SLOTS:
                 transpose_o(s + 1)
+                if s < 3:
+                    keep_warm(2)
                 transpose_g(s + 1)
+                transpose_go(s + 1)
             if s in (1, 2):
                 transpose_weights(s - 1, 0)
                 transpose_weights(s - 1, 1)
             if s + 2 < SLOTS:
                 transpose_y(s + 2)
-            if s + 1 < SLOTS:
-                transpose_go(s + 1)
-            if s >= 3:
-                multiply(s - 3)
+            multiplied = list(range(next_slot, min(next_slot + 2, s - 1))) if s >= 3 else []
+            for r in multiplied:
+                multiply(r)
+            next_slot += len(multiplied)
             if s + 3 < SLOTS:
                 natural(s + 3)
-            if s >= 3:
-                store(s - 3, False)
-        multiply(SLOTS - 3)
-        store(SLOTS - 3, False)
+        for r in multiplied:
+            store(r, False)
         quantise(SLOTS - 1, 1)
         multiply(SLOTS - 2)
         store(SLOTS - 2, False)

from contextlib import ExitStack

import concourse.mybir as mybir
from concourse.masks import make_identity

F32 = mybir.dt.float32
BF16 = mybir.dt.bfloat16
U32 = mybir.dt.uint32
U8 = mybir.dt.uint8
E5M2X4 = mybir.dt.float8_e5m2_x4
E4M3X4 = mybir.dt.float8_e4m3fn_x4
ALU = mybir.AluOpType
ACT = mybir.ActivationFunctionType

P = 128
PACK = 4
B = 2048
K = P * PACK
N = 512
SLOTS = B // P
WARM_UP = 4

FLOPS = 2 * 2 * B * K * N
BYTES = B * K * (2 + 4 + 4) + 2 * N * K * 2 + B * N * 4


def tile_gatel0rdcell_pb_v_kernel(tc, x_t, h_t, Wy, by, Wo, bo, y_hat, o_t, grad_out, out):
    nc = tc.nc
    y_rows = y_hat.rearrange("(p s) k -> p s k", s=SLOTS)
    o_rows = o_t.rearrange("(p s) k -> p s k", s=SLOTS)
    g_rows = grad_out.rearrange("(p s) k -> p s k", s=SLOTS)
    out_rows = out.rearrange("(p s) n -> p s n", s=SLOTS)

    with ExitStack() as stack:
        const = stack.enter_context(tc.tile_pool(name="const", bufs=1))
        inputs = stack.enter_context(tc.tile_pool(name="inputs", bufs=1))
        work = stack.enter_context(tc.tile_pool(name="work", bufs=3))
        codes_pool = stack.enter_context(tc.tile_pool(name="codes", bufs=5))
        results = stack.enter_context(tc.tile_pool(name="results", bufs=SLOTS))
        psum = stack.enter_context(tc.psum_pool(name="psum", bufs=2))
        stack.enter_context(tc.manual_schedule())

        zeros = const.tile([P, N], BF16, name="zeros")
        nc.vector.memset(zeros[:], 0.0)

        def keep_warm(count):
            warm_ps = psum.tile([P, N], F32, name="warm_ps", tag="acc", bufs=2)
            for i in range(count):
                nc.tensor.matmul(out=warm_ps[:], lhsT=zeros[:, 0:P], rhs=zeros[:], start=True, stop=True)

        keep_warm(WARM_UP)

        ident_f32 = const.tile([P, P], F32, name="ident_f32")
        make_identity(nc, ident_f32[:])
        ident_bf16 = const.tile([P, P], BF16, name="ident_bf16")
        make_identity(nc, ident_bf16[:])

        y_in, o_in, g_in = {}, {}, {}

        def load_slots(first, count):
            y_tile = inputs.tile([P, count, K], F32, name="y%d" % first)
            g_tile = inputs.tile([P, count, K], BF16, name="g%d" % first)
            o_tile = inputs.tile([P, count, K], F32, name="o%d" % first)
            nc.sync.dma_start(out=y_tile[:], in_=y_rows[:, first : first + count, :])
            nc.sync.dma_start(out=g_tile[:], in_=g_rows[:, first : first + count, :])
            nc.sync.dma_start(out=o_tile[:], in_=o_rows[:, first : first + count, :])
            for j in range(count):
                g_in[first + j] = g_tile[:, j, :]
                o_in[first + j] = o_tile[:, j, :]
                y_in[first + j] = y_tile[:, j, :]

        for s in range(4):
            load_slots(s, 1)
        w_raw = []
        for name, w in (("wy_raw", Wy), ("wo_raw", Wo)):
            raw = const.tile([P, N // P, K], BF16, name=name)
            nc.sync.dma_start(out=raw[:], in_=w[0:N, :].rearrange("(c i) k -> i c k", i=P))
            w_raw.append(raw)
        load_slots(4, 1)
        load_slots(5, 1)
        for first in range(6, SLOTS, 2):
            load_slots(first, 2)

        w_grouped = const.tile([P, 2, N // P, P, PACK], BF16, name="w_grouped", align_bytes=64)
        w_codes = const.tile([P, 2 * N], U32, name="w_codes", align_bytes=64)
        w_scales = const.tile([P, 2 * N], U8, name="w_scales", align_bytes=64)

        def transpose_weights(z, part):
            w_t = psum.tile([P, 2, PACK, P], BF16, name="w_t", tag="acc", bufs=2)
            for h in range(2):
                for t in range(PACK):
                    nc.tensor.transpose(
                        out=w_t[:, h, t, :],
                        in_=w_raw[z][:, 2 * part + h, t * P : (t + 1) * P],
                        identity=ident_bf16[:],
                    )
            nc.scalar.copy(out=w_grouped[:, z, 2 * part : 2 * part + 2], in_=w_t[:].rearrange("p h t i -> p h i t"))

        def quantise_weights():
            nc.vector.quantize_mx(
                out=w_codes[:].bitcast(E4M3X4),
                scales=w_scales[:],
                in_=w_grouped[:].rearrange("p z c i t -> p (z c i t)"),
            )

        go, goy, ysq, y_sb, goy_sb, u, yo, g_ps, o_ps, go_ps = {}, {}, {}, {}, {}, {}, {}, {}, {}, {}
        grouped, dz_codes, dz_scales, acc = {}, {}, {}, {}

        def by_word(ps):
            return ps[:].rearrange("p t b -> p b t")

        def transpose_to(dst, src):
            for t in range(PACK):
                nc.tensor.transpose(out=dst[:, t, :], in_=src[:, t * P : (t + 1) * P], identity=ident_f32[:])

        def on_vector(s):
            return s < 8 or s % 2 == 0

        def natural(s):
            go[s] = work.tile([P, K], F32, name="go", bufs=6)
            nc.gpsimd.tensor_tensor(out=go[s][:], in0=g_in[s], in1=o_in[s], op=ALU.mult)
            if not on_vector(s):
                goy[s] = work.tile([P, K], F32, name="goy", bufs=6)
                nc.gpsimd.tensor_tensor(out=goy[s][:], in0=go[s][:], in1=y_in[s], op=ALU.mult)

        def transpose_y(s):
            y_ps = psum.tile([P, PACK, P], F32, name="y_ps", bufs=1)
            transpose_to(y_ps, y_in[s])
            ysq[s] = work.tile([P, P, PACK], F32, name="ysq")
            nc.scalar.activation(out=ysq[s][:], in_=by_word(y_ps), func=ACT.Square)
            if on_vector(s):
                y_sb[s] = work.tile([P, P, PACK], F32, name="y_sb")
                nc.scalar.copy(out=y_sb[s][:], in_=by_word(y_ps))

        def transpose_g(s):
            g_ps[s] = psum.tile([P, PACK, P], BF16, name="g_ps", bufs=1)
            for t in range(PACK):
                nc.tensor.transpose(out=g_ps[s][:, t, :], in_=g_in[s][:, t * P : (t + 1) * P], identity=ident_bf16[:])

        def transpose_o(s):
            o_ps[s] = psum.tile([P, PACK, P], F32, name="o_ps")
            transpose_to(o_ps[s], o_in[s])

        def transpose_go(s):
            go_ps[s] = psum.tile([P, PACK, P], F32, name="go_ps")
            transpose_to(go_ps[s], go[s] if on_vector(s) else goy[s])
            if not on_vector(s):
                goy_sb[s] = work.tile([P, P, PACK], F32, name="goy_sb")
                nc.scalar.copy(out=goy_sb[s][:], in_=by_word(go_ps[s]))

        def factors(s):
            u[s] = work.tile([P, P, PACK], F32, name="u")
            nc.vector.scalar_tensor_tensor(
                out=u[s][:], in0=ysq[s][:], scalar=1.0, in1=by_word(g_ps[s]), op0=ALU.subtract, op1=ALU.mult
            )
            if on_vector(s):
                yo[s] = work.tile([P, P, PACK], F32, name="yo")
                nc.vector.scalar_tensor_tensor(
                    out=yo[s][:], in0=by_word(o_ps[s]), scalar=1.0, in1=y_sb[s][:], op0=ALU.subtract, op1=ALU.mult
                )

        def gradients(s):
            q, half = divmod(s, 2)
            if half == 0:
                grouped[q] = work.tile([P, 2, 2, P, PACK], BF16, name="grouped", align_bytes=64)
            if not on_vector(s):
                nc.vector.scalar_tensor_tensor(
                    out=grouped[q][:, half, 1], in0=by_word(o_ps[s]), scalar=1.0, in1=goy_sb[s][:],
                    op0=ALU.subtract, op1=ALU.mult,
                )
            nc.vector.tensor_tensor(out=grouped[q][:, half, 0], in0=u[s][:], in1=by_word(o_ps[s]), op=ALU.mult)
            if on_vector(s):
                nc.vector.tensor_tensor(out=grouped[q][:, half, 1], in0=yo[s][:], in1=by_word(go_ps[s]), op=ALU.mult)

        def quantise(first, count):
            q, half = divmod(first, 2)
            if half == 0:
                dz_codes[q] = codes_pool.tile([P, 4 * P], U32, name="dz_codes", align_bytes=64)
                dz_scales[q] = codes_pool.tile([P, 4 * P], U8, name="dz_scales", align_bytes=64)
            cols = slice(half * 2 * P, (half + count) * 2 * P)
            nc.vector.quantize_mx(
                out=dz_codes[q][:, cols].bitcast(E5M2X4),
                scales=dz_scales[q][:, cols],
                in_=grouped[q][:, half : half + count].rearrange("p h z b t -> p (h z b t)"),
            )

        def multiply(s):
            q, half = divmod(s, 2)
            acc[s] = psum.tile([P, N], F32, name="acc", bufs=2)
            for z in range(2):
                cols = slice((2 * half + z) * P, (2 * half + z + 1) * P)
                w_cols = slice(z * N, (z + 1) * N)
                nc.tensor.matmul_mx(
                    out=acc[s][:],
                    lhsT=dz_codes[q][:, cols].bitcast(E5M2X4),
                    lhsT_scale=dz_scales[q][:, cols],
                    rhs=w_codes[:, w_cols].bitcast(E4M3X4),
                    rhs_scale=w_scales[:, w_cols],
                    start=(z == 0),
                    stop=(z == 1),
                )

        def store(s, on_vector):
            out_sb = results.tile([P, N], F32, name="out_sb")
            if on_vector:
                nc.vector.tensor_scalar_mul(out=out_sb[:], in0=acc[s][:], scalar1=-1.0)
            else:
                nc.scalar.mul(out=out_sb[:], in_=acc[s][:], mul=-1.0)
            nc.sync.dma_start(out=out_rows[:, s, :], in_=out_sb[:])

        natural(0)
        natural(1)
        transpose_y(0)
        transpose_o(0)
        keep_warm(2)
        transpose_g(0)
        transpose_go(0)
        transpose_y(1)
        natural(2)
        multiplied = []
        next_slot = 0
        for s in range(SLOTS):
            factors(s)
            if s >= 2 and s % 2 == 0:
                quantise(s - 2, 2)
            if s == SLOTS - 1:
                quantise(s - 1, 1)
            gradients(s)
            if s == 3:
                quantise_weights()
            for r in multiplied:
                store(r, False)
            if s + 1 < SLOTS:
                transpose_o(s + 1)
                if s < 3:
                    keep_warm(2)
                transpose_g(s + 1)
                transpose_go(s + 1)
            if s in (1, 2):
                transpose_weights(s - 1, 0)
                transpose_weights(s - 1, 1)
            if s + 2 < SLOTS:
                transpose_y(s + 2)
            multiplied = list(range(next_slot, min(next_slot + 2, s - 1))) if s >= 3 else []
            for r in multiplied:
                multiply(r)
            next_slot += len(multiplied)
            if s + 3 < SLOTS:
                natural(s + 3)
        for r in multiplied:
            store(r, False)
        quantise(SLOTS - 1, 1)
        multiply(SLOTS - 2)
        store(SLOTS - 2, False)
        multiply(SLOTS - 1)
        store(SLOTS - 1, True)
